import numpy as np
import ml_dtypes


def mxq(x, axis, fmt="e4m3"):
    dtype, down = {"e4m3": (ml_dtypes.float8_e4m3fn, 7), "e5m2": (ml_dtypes.float8_e5m2, 14)}[fmt]
    v = np.moveaxis(np.asarray(x, np.float32).astype(ml_dtypes.bfloat16).astype(np.float64), axis, -1)
    blocks = v.reshape(v.shape[:-1] + (-1, 32))
    amax = np.abs(blocks).max(-1, keepdims=True)
    byte = np.maximum(np.where(amax > 0, np.frexp(amax)[1] - 1 + 127, 0) - down, 1)
    scale = np.exp2(byte - 127.0)
    codes = (blocks / scale).astype(np.float32).astype(dtype).astype(np.float64)
    return np.moveaxis((codes * scale).reshape(v.shape), -1, axis)


WIDE = False


def mx_kscale(k):
    if not WIDE:
        return np.ones(k)
    levels = np.array([10, -10, 5, -5, 0])
    a = np.random.permutation(np.resize(levels, k // 512 * 4)).reshape(k // 512, 4)
    idx = np.arange(k)
    return np.exp2(a[idx // 512, idx % 128 // 32])


BF16 = ml_dtypes.bfloat16


def bf(x):
    return np.asarray(x, np.float32).astype(BF16)


def f64(x):
    return np.asarray(x).astype(np.float64)


M, N, H, D, P = 8192, 512, 2, 64, 1024
E = H * D


def rms_norm(x):
    return x * (1.0 / np.sqrt(np.mean(x * x, axis=-1, keepdims=True)))


def setup_inputs():
    s = mx_kscale(N)
    c = np.sqrt(np.mean(s * s))
    r = np.exp2(np.random.uniform(-1.0, 1.0, (M, 1)))
    return {"X": bf(np.random.standard_normal((M, N)) * r * s),
            "W_q": bf(np.random.standard_normal((N, E)) * 2.0 / np.sqrt(N) / s[:, None] * c),
            "W_k": bf(np.random.standard_normal((N, E)) * 0.5 / np.sqrt(N) / s[:, None] * c),
            "W_v": bf(np.random.standard_normal((N, E)) * 1.0 / np.sqrt(N) / s[:, None] * c)}


def reference(X, W_q, W_k, W_v):
    xq = mxq(rms_norm(f64(X)), 1, "e4m3")
    q = (xq @ mxq(f64(W_q), 0, "e4m3")).reshape(M, H, D)
    k = (xq @ mxq(f64(W_k), 0, "e4m3")).reshape(M, H, D)
    v = (xq @ mxq(f64(W_v), 0, "e4m3")).reshape(M, H, D)
    qn = rms_norm(q)
    kn = rms_norm(k)
    return qn, kn.transpose(1, 0, 2), v.transpose(1, 0, 2)

@@ -1,0 +1,187 @@
+from contextlib import ExitStack
+
+import concourse.mybir as mybir
+from concourse.masks import make_identity
+
+BF16 = mybir.dt.bfloat16
+F32 = mybir.dt.float32
+U32 = mybir.dt.uint32
+U8 = mybir.dt.uint8
+FP8X4 = mybir.dt.float8_e4m3fn_x4
+ACT = mybir.ActivationFunctionType
+ALU = mybir.AluOpType
+
+P = 128
+ROWS = 8192
+FEATURES = 512
+HEADS = 2
+HEAD_DIM = 64
+WIDTH = HEADS * HEAD_DIM
+TILES = ROWS // P
+GROUP = 4
+GROUPS = TILES // GROUP
+PAIR = 2
+
+FLOPS = 2 * ROWS * FEATURES * 3 * WIDTH
+
+
+def tile_flashinfer_normqknorm_pa_t_kernel(tc, X, W_q, W_k, W_v, out_0, out_1, out_2):
+    nc = tc.nc
+    x_rows = X.rearrange("(p t) k -> p t k", t=TILES)
+    q_rows = out_0.rearrange("(p t) h d -> p t (h d)", t=TILES)
+    k_rows = out_1.rearrange("h (p t) d -> p h t d", t=TILES)
+    v_rows = out_2.rearrange("h (p t) d -> p h t d", t=TILES)
+
+    with ExitStack() as ctx:
+        const = ctx.enter_context(tc.tile_pool(name="const", bufs=1))
+        xin = ctx.enter_context(tc.tile_pool(name="xin", bufs=GROUPS))
+        work = ctx.enter_context(tc.tile_pool(name="work", bufs=2))
+        small = ctx.enter_context(tc.tile_pool(name="small", bufs=3))
+        outs = ctx.enter_context(tc.tile_pool(name="outs", bufs=4))
+        psum = ctx.enter_context(tc.psum_pool(name="psum", bufs=2))
+
+        ident = const.tile([P, P], F32)
+        make_identity(nc, ident[:])
+
+        x_sb, rms, xn, xt, grouped = {}, {}, {}, {}, {}
+        x_codes, x_scales, acc, head_rms = {}, {}, {}, {}
+
+        def load(g):
+            x_sb[g] = xin.tile([P, GROUP, FEATURES], BF16, name="x_sb")
+            nc.sync.dma_start(out=x_sb[g][:], in_=x_rows[:, g * GROUP : (g + 1) * GROUP, :])
+
+        load(0)
+        w_raw = const.tile([P, 3, 4, WIDTH], BF16)
+        for w, weight in enumerate((W_q, W_k, W_v)):
+            nc.sync.dma_start(
+                out=w_raw[:, w, :, :].rearrange("p (u e) n -> p u e n", u=2),
+                in_=weight.rearrange("(u p e) n -> p u e n", u=2, e=2),
+            )
+        for g in range(1, GROUPS):
+            load(g)
+
+        w_grouped = const.tile([P, 3, WIDTH, 4], BF16, align_bytes=64)
+        nc.vector.tensor_copy(out=w_grouped[:], in_=w_raw[:].rearrange("p w t n -> p w n t"))
+        w_codes = const.tile([P, 3, WIDTH], U32, align_bytes=64)
+        w_scales = const.tile([P, 3, WIDTH], U8, align_bytes=64)
+        for w in range(3):
+            nc.vector.quantize_mx(
+                out=w_codes[:, w, :].bitcast(FP8X4),
+                scales=w_scales[:, w, :],
+                in_=w_grouped[:, w, :, :].rearrange("p n t -> p (n t)"),
+            )
+
+        def row_stats(g):
+            squares = work.tile([P, GROUP, FEATURES], BF16, name="squares")
+            sum_sq = small.tile([P, GROUP], F32, name="sum_sq")
+            for j in range(GROUP):
+                nc.scalar.activation(
+                    out=squares[:, j, :], in_=x_sb[g][:, j, :], func=ACT.Square,
+                    accum_out=sum_sq[:, j : j + 1],
+                )
+            rms[g] = small.tile([P, GROUP], F32, name="rms")
+            nc.scalar.activation(out=rms[g][:], in_=sum_sq[:], func=ACT.Sqrt, scale=1.0 / FEATURES)
+
+        def normalise(g):
+            inv_rms = small.tile([P, GROUP], F32, name="inv_rms")
+            nc.vector.reciprocal(out=inv_rms[:], in_=rms[g][:])
+            xn[g] = work.tile([P, GROUP, FEATURES], BF16, name="xn")
+            for j in range(GROUP):
+                nc.vector.tensor_scalar_mul(
+                    out=xn[g][:, j, :], in0=x_sb[g][:, j, :], scalar1=inv_rms[:, j : j + 1]
+                )
+
+        def transpose(g):
+            xt[g] = []
+            for j0 in range(0, GROUP, PAIR):
+                bank = psum.tile([P, PAIR, 2, P], F32, name="xt")
+                for jj in range(PAIR):
+                    words = xn[g][:, j0 + jj, :].bitcast(F32)
+                    for u in range(2):
+                        nc.tensor.transpose(bank[:, jj, u, :], words[:, u * P : (u + 1) * P], ident[:])
+                xt[g].append(bank)
+
+        def regroup(g):
+            grouped[g] = work.tile([P, GROUP, P, 4], BF16, name="grouped", align_bytes=64)
+            for b, bank in enumerate(xt[g]):
+                nc.vector.tensor_copy(
+                    out=grouped[g][:, b * PAIR : (b + 1) * PAIR, :, :].bitcast(F32),
+                    in_=bank[:].rearrange("p j u r -> p j r u"),
+                )
+
+        def quantise(g):
+            x_codes[g] = work.tile([P, GROUP, P], U32, name="x_codes", align_bytes=64)
+            x_scales[g] = work.tile([P, GROUP, P], U8, name="x_scales", align_bytes=64)
+            nc.vector.quantize_mx(
+                out=x_codes[g][:].rearrange("p j r -> p (j r)").bitcast(FP8X4),
+                scales=x_scales[g][:].rearrange("p j r -> p (j r)"),
+                in_=grouped[g][:].rearrange("p j r t -> p (j r t)"),
+            )
+
+        def project(g):
+            acc[g] = []
+            for w, name in enumerate(("acc_q", "acc_k", "acc_v")):
+                bank = psum.tile([P, GROUP, HEADS, HEAD_DIM], F32, name=name)
+                for j in range(GROUP):
+                    nc.tensor.matmul_mx(
+                        out=bank[:, j, :, :].rearrange("p h d -> p (h d)"),
+                        lhsT=x_codes[g][:, j, :].bitcast(FP8X4),
+                        lhsT_scale=x_scales[g][:, j, :],
+                        rhs=w_codes[:, w, :].bitcast(FP8X4),
+                        rhs_scale=w_scales[:, w, :],
+                        start=True,
+                        stop=True,
+                    )
+                acc[g].append(bank)
+
+        def head_stats(g):
+            head_sq = work.tile([P, 2, GROUP, HEADS, HEAD_DIM], BF16, name="head_sq")
+            head_sum = small.tile([P, 2, GROUP, HEADS], F32, name="head_sum")
+            for a in range(2):
+                for j in range(GROUP):
+                    for h in range(HEADS):
+                        nc.scalar.activation(
+                            out=head_sq[:, a, j, h, :], in_=acc[g][a][:, j, h, :], func=ACT.Square,
+                            accum_out=head_sum[:, a, j, h : h + 1],
+                        )
+            head_rms[g] = small.tile([P, 2, GROUP, HEADS], F32, name="head_rms")
+            nc.scalar.activation(
+                out=head_rms[g][:], in_=head_sum[:], func=ACT.Sqrt, scale=1.0 / HEAD_DIM
+            )
+
+        def finish(g):
+            acc_q, acc_k, acc_v = acc[g]
+            tiles = slice(g * GROUP, (g + 1) * GROUP)
+            full = [P, GROUP, HEADS, HEAD_DIM]
+            head_inv = small.tile([P, 2, GROUP, HEADS], F32, name="head_inv")
+            nc.vector.reciprocal(out=head_inv[:], in_=head_rms[g][:])
+            q_sb = outs.tile([P, GROUP, HEADS, HEAD_DIM], F32, name="q_sb")
+            nc.vector.tensor_tensor(
+                out=q_sb[:], in0=acc_q[:],
+                in1=head_inv[:, 0].unsqueeze(3).to_broadcast(full), op=ALU.mult,
+            )
+            nc.sync.dma_start(out=q_rows[:, tiles, :], in_=q_sb[:].rearrange("p j h d -> p j (h d)"))
+            k_sb = outs.tile([P, HEADS, GROUP, HEAD_DIM], F32, name="k_sb")
+            nc.vector.tensor_tensor(
+                out=k_sb[:].rearrange("p h j d -> p j h d"), in0=acc_k[:],
+                in1=head_inv[:, 1].unsqueeze(3).to_broadcast(full), op=ALU.mult,
+            )
+            nc.sync.dma_start(out=k_rows[:, :, tiles, :], in_=k_sb[:])
+            v_sb = outs.tile([P, HEADS, GROUP, HEAD_DIM], F32, name="v_sb")
+            nc.vector.tensor_copy(out=v_sb[:].rearrange("p h j d -> p j h d"), in_=acc_v[:])
+            nc.sync.dma_start(out=v_rows[:, :, tiles, :], in_=v_sb[:])
+
+        def run(stage, g):
+            if 0 <= g < GROUPS:
+                stage(g)
+
+        ctx.enter_context(tc.manual_schedule())
+        for i in range(-2, GROUPS + 1):
+            run(row_stats, i + 2)
+            run(normalise, i + 1)
+            run(transpose, i + 1)
+            run(quantise, i)
+            run(project, i)
+            run(finish, i - 1)
+            run(regroup, i + 1)
+            run(head_stats, i)

@@ -44,7 +44,7 @@ def tile_flashinfer_normqknorm_pa_t_kernel(tc, X, W_q, W_k, W_v, out_0, out_1, o
         make_identity(nc, ident[:])
 
         x_sb, rms, xn, xt, grouped = {}, {}, {}, {}, {}
-        x_codes, x_scales, acc, head_rms = {}, {}, {}, {}
+        x_codes, x_scales, acc, head_ms, head_rms = {}, {}, {}, {}, {}
 
         def load(g):
             x_sb[g] = xin.tile([P, GROUP, FEATURES], BF16, name="x_sb")
@@ -59,17 +59,18 @@ def tile_flashinfer_normqknorm_pa_t_kernel(tc, X, W_q, W_k, W_v, out_0, out_1, o
             )
         for g in range(1, GROUPS):
             load(g)
-
-        w_grouped = const.tile([P, 3, WIDTH, 4], BF16, align_bytes=64)
-        nc.vector.tensor_copy(out=w_grouped[:], in_=w_raw[:].rearrange("p w t n -> p w n t"))
         w_codes = const.tile([P, 3, WIDTH], U32, align_bytes=64)
         w_scales = const.tile([P, 3, WIDTH], U8, align_bytes=64)
-        for w in range(3):
-            nc.vector.quantize_mx(
-                out=w_codes[:, w, :].bitcast(FP8X4),
-                scales=w_scales[:, w, :],
-                in_=w_grouped[:, w, :, :].rearrange("p n t -> p (n t)"),
-            )
+
+        def quantise_weights():
+            w_grouped = const.tile([P, 3, WIDTH, 4], BF16, align_bytes=64)
+            nc.vector.tensor_copy(out=w_grouped[:], in_=w_raw[:].rearrange("p w t n -> p w n t"))
+            for w in range(3):
+                nc.vector.quantize_mx(
+                    out=w_codes[:, w, :].bitcast(FP8X4),
+                    scales=w_scales[:, w, :],
+                    in_=w_grouped[:, w, :, :].rearrange("p n t -> p (n t)"),
+                )
 
         def row_stats(g):
             squares = work.tile([P, GROUP, FEATURES], BF16, name="squares")
@@ -104,7 +105,7 @@ def tile_flashinfer_normqknorm_pa_t_kernel(tc, X, W_q, W_k, W_v, out_0, out_1, o
         def regroup(g):
             grouped[g] = work.tile([P, GROUP, P, 4], BF16, name="grouped", align_bytes=64)
             for b, bank in enumerate(xt[g]):
-                nc.vector.tensor_copy(
+                nc.scalar.copy(
                     out=grouped[g][:, b * PAIR : (b + 1) * PAIR, :, :].bitcast(F32),
                     in_=bank[:].rearrange("p j u r -> p j r u"),
                 )
@@ -135,53 +136,69 @@ def tile_flashinfer_normqknorm_pa_t_kernel(tc, X, W_q, W_k, W_v, out_0, out_1, o
                 acc[g].append(bank)
 
         def head_stats(g):
-            head_sq = work.tile([P, 2, GROUP, HEADS, HEAD_DIM], BF16, name="head_sq")
-            head_sum = small.tile([P, 2, GROUP, HEADS], F32, name="head_sum")
+            moments = small.tile([P, 2, GROUP, HEADS, 3], F32, name="moments")
             for a in range(2):
                 for j in range(GROUP):
-                    for h in range(HEADS):
-                        nc.scalar.activation(
-                            out=head_sq[:, a, j, h, :], in_=acc[g][a][:, j, h, :], func=ACT.Square,
-                            accum_out=head_sum[:, a, j, h : h + 1],
-                        )
-            head_rms[g] = small.tile([P, 2, GROUP, HEADS], F32, name="head_rms")
-            nc.scalar.activation(
-                out=head_rms[g][:], in_=head_sum[:], func=ACT.Sqrt, scale=1.0 / HEAD_DIM
+                    nc.vector.bn_stats(
+                        out=moments[:, a, j, :, :].rearrange("p h s -> p (h s)"),
+                        in_=acc[g][a][:, j, :, :].rearrange("p h d -> p d h"),
+                    )
+            mean_sq = small.tile([P, 2, GROUP, HEADS], F32, name="mean_sq")
+            nc.vector.tensor_tensor(
+                out=mean_sq[:], in0=moments[:, :, :, :, 1], in1=moments[:, :, :, :, 1], op=ALU.mult
+            )
+            head_ms[g] = small.tile([P, 2, GROUP, HEADS], F32, name="head_ms")
+            nc.vector.scalar_tensor_tensor(
+                out=head_ms[g][:], in0=moments[:, :, :, :, 2], scalar=1.0 / HEAD_DIM,
+                in1=mean_sq[:], op0=ALU.mult, op1=ALU.add,
             )
 
+        def head_root(g):
+            head_rms[g] = small.tile([P, 2, GROUP, HEADS], F32, name="head_rms")
+            nc.scalar.activation(out=head_rms[g][:], in_=head_ms[g][:], func=ACT.Sqrt)
+
+        def store_v(g):
+            v_sb = outs.tile([P, HEADS, GROUP, HEAD_DIM], F32, name="v_sb")
+            nc.scalar.copy(out=v_sb[:].rearrange("p h j d -> p j h d"), in_=acc[g][2][:])
+            nc.sync.dma_start(out=v_rows[:, :, g * GROUP : (g + 1) * GROUP, :], in_=v_sb[:])
+
         def finish(g):
-            acc_q, acc_k, acc_v = acc[g]
             tiles = slice(g * GROUP, (g + 1) * GROUP)
             full = [P, GROUP, HEADS, HEAD_DIM]
             head_inv = small.tile([P, 2, GROUP, HEADS], F32, name="head_inv")
             nc.vector.reciprocal(out=head_inv[:], in_=head_rms[g][:])
             q_sb = outs.tile([P, GROUP, HEADS, HEAD_DIM], F32, name="q_sb")
             nc.vector.tensor_tensor(
-                out=q_sb[:], in0=acc_q[:],
+                out=q_sb[:], in0=acc[g][0][:],
                 in1=head_inv[:, 0].unsqueeze(3).to_broadcast(full), op=ALU.mult,
             )
             nc.sync.dma_start(out=q_rows[:, tiles, :], in_=q_sb[:].rearrange("p j h d -> p j (h d)"))
             k_sb = outs.tile([P, HEADS, GROUP, HEAD_DIM], F32, name="k_sb")
             nc.vector.tensor_tensor(
-                out=k_sb[:].rearrange("p h j d -> p j h d"), in0=acc_k[:],
+                out=k_sb[:].rearrange("p h j d -> p j h d"), in0=acc[g][1][:],
                 in1=head_inv[:, 1].unsqueeze(3).to_broadcast(full), op=ALU.mult,
             )
             nc.sync.dma_start(out=k_rows[:, :, tiles, :], in_=k_sb[:])
-            v_sb = outs.tile([P, HEADS, GROUP, HEAD_DIM], F32, name="v_sb")
-            nc.vector.tensor_copy(out=v_sb[:].rearrange("p h j d -> p j h d"), in_=acc_v[:])
-            nc.sync.dma_start(out=v_rows[:, :, tiles, :], in_=v_sb[:])
 
         def run(stage, g):
             if 0 <= g < GROUPS:
                 stage(g)
 
         ctx.enter_context(tc.manual_schedule())
-        for i in range(-2, GROUPS + 1):
+        row_stats(0)
+        row_stats(1)
+        normalise(0)
+        transpose(0)
+        quantise_weights()
+        regroup(0)
+        for i in range(GROUPS + 2):
+            run(head_root, i - 1)
             run(row_stats, i + 2)
-            run(normalise, i + 1)
-            run(transpose, i + 1)
             run(quantise, i)
             run(project, i)
+            run(normalise, i + 1)
+            run(transpose, i + 1)
             run(finish, i - 1)
-            run(regroup, i + 1)
             run(head_stats, i)
+            run(regroup, i + 1)
+            run(store_v, i)

@@ -39,12 +39,13 @@ def tile_flashinfer_normqknorm_pa_t_kernel(tc, X, W_q, W_k, W_v, out_0, out_1, o
         small = ctx.enter_context(tc.tile_pool(name="small", bufs=3))
         outs = ctx.enter_context(tc.tile_pool(name="outs", bufs=4))
         psum = ctx.enter_context(tc.psum_pool(name="psum", bufs=2))
+        ctx.enter_context(tc.manual_schedule())
 
         ident = const.tile([P, P], F32)
         make_identity(nc, ident[:])
 
-        x_sb, rms, xn, xt, grouped = {}, {}, {}, {}, {}
-        x_codes, x_scales, acc, head_ms, head_rms = {}, {}, {}, {}, {}
+        x_sb, squares, sum_sq, rms, inv_rms, xn, xt, grouped = {}, {}, {}, {}, {}, {}, {}, {}
+        x_codes, x_scales, acc, moments, mean_sq, head_ms, head_rms, head_inv = {}, {}, {}, {}, {}, {}, {}, {}
 
         def load(g):
             x_sb[g] = xin.tile([P, GROUP, FEATURES], BF16, name="x_sb")
@@ -59,37 +60,40 @@ def tile_flashinfer_normqknorm_pa_t_kernel(tc, X, W_q, W_k, W_v, out_0, out_1, o
             )
         for g in range(1, GROUPS):
             load(g)
+        w_grouped = const.tile([P, 3, WIDTH, 4], BF16, align_bytes=64)
+        nc.vector.tensor_copy(out=w_grouped[:], in_=w_raw[:].rearrange("p w t n -> p w n t"))
         w_codes = const.tile([P, 3, WIDTH], U32, align_bytes=64)
         w_scales = const.tile([P, 3, WIDTH], U8, align_bytes=64)
+        for w in range(3):
+            nc.vector.quantize_mx(
+                out=w_codes[:, w, :].bitcast(FP8X4),
+                scales=w_scales[:, w, :],
+                in_=w_grouped[:, w, :, :].rearrange("p n t -> p (n t)"),
+            )
 
-        def quantise_weights():
-            w_grouped = const.tile([P, 3, WIDTH, 4], BF16, align_bytes=64)
-            nc.vector.tensor_copy(out=w_grouped[:], in_=w_raw[:].rearrange("p w t n -> p w n t"))
-            for w in range(3):
-                nc.vector.quantize_mx(
-                    out=w_codes[:, w, :].bitcast(FP8X4),
-                    scales=w_scales[:, w, :],
-                    in_=w_grouped[:, w, :, :].rearrange("p n t -> p (n t)"),
-                )
-
-        def row_stats(g):
-            squares = work.tile([P, GROUP, FEATURES], BF16, name="squares")
-            sum_sq = small.tile([P, GROUP], F32, name="sum_sq")
-            for j in range(GROUP):
+        def row_squares(g, tiles):
+            if g not in sum_sq:
+                squares[g] = work.tile([P, GROUP, FEATURES], BF16, name="squares")
+                sum_sq[g] = small.tile([P, GROUP], F32, name="sum_sq")
+            for j in tiles:
                 nc.scalar.activation(
-                    out=squares[:, j, :], in_=x_sb[g][:, j, :], func=ACT.Square,
-                    accum_out=sum_sq[:, j : j + 1],
+                    out=squares[g][:, j, :], in_=x_sb[g][:, j, :], func=ACT.Square,
+                    accum_out=sum_sq[g][:, j : j + 1],
                 )
+
+        def row_root(g):
             rms[g] = small.tile([P, GROUP], F32, name="rms")
-            nc.scalar.activation(out=rms[g][:], in_=sum_sq[:], func=ACT.Sqrt, scale=1.0 / FEATURES)
+            nc.scalar.activation(out=rms[g][:], in_=sum_sq[g][:], func=ACT.Sqrt, scale=1.0 / FEATURES)
+
+        def invert_row_rms(g):
+            inv_rms[g] = small.tile([P, GROUP], F32, name="inv_rms")
+            nc.vector.reciprocal(out=inv_rms[g][:], in_=rms[g][:])
 
         def normalise(g):
-            inv_rms = small.tile([P, GROUP], F32, name="inv_rms")
-            nc.vector.reciprocal(out=inv_rms[:], in_=rms[g][:])
             xn[g] = work.tile([P, GROUP, FEATURES], BF16, name="xn")
             for j in range(GROUP):
                 nc.vector.tensor_scalar_mul(
-                    out=xn[g][:, j, :], in0=x_sb[g][:, j, :], scalar1=inv_rms[:, j : j + 1]
+                    out=xn[g][:, j, :], in0=x_sb[g][:, j, :], scalar1=inv_rms[g][:, j : j + 1]
                 )
 
         def transpose(g):
@@ -135,70 +139,80 @@ def tile_flashinfer_normqknorm_pa_t_kernel(tc, X, W_q, W_k, W_v, out_0, out_1, o
                     )
                 acc[g].append(bank)
 
-        def head_stats(g):
-            moments = small.tile([P, 2, GROUP, HEADS, 3], F32, name="moments")
+        def head_moments(g):
+            moments[g] = small.tile([P, 2, GROUP, HEADS, 3], F32, name="moments")
             for a in range(2):
                 for j in range(GROUP):
                     nc.vector.bn_stats(
-                        out=moments[:, a, j, :, :].rearrange("p h s -> p (h s)"),
+                        out=moments[g][:, a, j, :, :].rearrange("p h s -> p (h s)"),
                         in_=acc[g][a][:, j, :, :].rearrange("p h d -> p d h"),
                     )
-            mean_sq = small.tile([P, 2, GROUP, HEADS], F32, name="mean_sq")
-            nc.vector.tensor_tensor(
-                out=mean_sq[:], in0=moments[:, :, :, :, 1], in1=moments[:, :, :, :, 1], op=ALU.mult
-            )
+
+        def square_head_means(g):
+            mean = moments[g][:, :, :, :, 1]
+            mean_sq[g] = small.tile([P, 2, GROUP, HEADS], F32, name="mean_sq")
+            nc.vector.tensor_tensor(out=mean_sq[g][:], in0=mean, in1=mean, op=ALU.mult)
+
+        def head_mean_squares(g):
             head_ms[g] = small.tile([P, 2, GROUP, HEADS], F32, name="head_ms")
             nc.vector.scalar_tensor_tensor(
-                out=head_ms[g][:], in0=moments[:, :, :, :, 2], scalar=1.0 / HEAD_DIM,
-                in1=mean_sq[:], op0=ALU.mult, op1=ALU.add,
+                out=head_ms[g][:], in0=moments[g][:, :, :, :, 2], scalar=1.0 / HEAD_DIM,
+                in1=mean_sq[g][:], op0=ALU.mult, op1=ALU.add,
             )
 
         def head_root(g):
             head_rms[g] = small.tile([P, 2, GROUP, HEADS], F32, name="head_rms")
             nc.scalar.activation(out=head_rms[g][:], in_=head_ms[g][:], func=ACT.Sqrt)
 
-        def store_v(g):
-            v_sb = outs.tile([P, HEADS, GROUP, HEAD_DIM], F32, name="v_sb")
-            nc.scalar.copy(out=v_sb[:].rearrange("p h j d -> p j h d"), in_=acc[g][2][:])
-            nc.sync.dma_start(out=v_rows[:, :, g * GROUP : (g + 1) * GROUP, :], in_=v_sb[:])
+        def invert_head_rms(g):
+            head_inv[g] = small.tile([P, 2, GROUP, HEADS], F32, name="head_inv")
+            nc.vector.reciprocal(out=head_inv[g][:], in_=head_rms[g][:])
 
-        def finish(g):
-            tiles = slice(g * GROUP, (g + 1) * GROUP)
-            full = [P, GROUP, HEADS, HEAD_DIM]
-            head_inv = small.tile([P, 2, GROUP, HEADS], F32, name="head_inv")
-            nc.vector.reciprocal(out=head_inv[:], in_=head_rms[g][:])
+        def store_q(g):
             q_sb = outs.tile([P, GROUP, HEADS, HEAD_DIM], F32, name="q_sb")
             nc.vector.tensor_tensor(
                 out=q_sb[:], in0=acc[g][0][:],
-                in1=head_inv[:, 0].unsqueeze(3).to_broadcast(full), op=ALU.mult,
+                in1=head_inv[g][:, 0].unsqueeze(3).to_broadcast([P, GROUP, HEADS, HEAD_DIM]),
+                op=ALU.mult,
             )
-            nc.sync.dma_start(out=q_rows[:, tiles, :], in_=q_sb[:].rearrange("p j h d -> p j (h d)"))
+            nc.sync.dma_start(
+                out=q_rows[:, g * GROUP : (g + 1) * GROUP, :],
+                in_=q_sb[:].rearrange("p j h d -> p j (h d)"),
+            )
+
+        def store_k(g):
             k_sb = outs.tile([P, HEADS, GROUP, HEAD_DIM], F32, name="k_sb")
             nc.vector.tensor_tensor(
                 out=k_sb[:].rearrange("p h j d -> p j h d"), in0=acc[g][1][:],
-                in1=head_inv[:, 1].unsqueeze(3).to_broadcast(full), op=ALU.mult,
+                in1=head_inv[g][:, 1].unsqueeze(3).to_broadcast([P, GROUP, HEADS, HEAD_DIM]),
+                op=ALU.mult,
             )
-            nc.sync.dma_start(out=k_rows[:, :, tiles, :], in_=k_sb[:])
+            nc.sync.dma_start(out=k_rows[:, :, g * GROUP : (g + 1) * GROUP, :], in_=k_sb[:])
 
-        def run(stage, g):
+        def store_v(g):
+            v_sb = outs.tile([P, HEADS, GROUP, HEAD_DIM], F32, name="v_sb")
+            nc.vector.tensor_copy(out=v_sb[:].rearrange("p h j d -> p j h d"), in_=acc[g][2][:])
+            nc.sync.dma_start(out=v_rows[:, :, g * GROUP : (g + 1) * GROUP, :], in_=v_sb[:])
+
+        def run(stage, g, *args):
             if 0 <= g < GROUPS:
-                stage(g)
+                stage(g, *args)
 
-        ctx.enter_context(tc.manual_schedule())
-        row_stats(0)
-        row_stats(1)
-        normalise(0)
-        transpose(0)
-        quantise_weights()
-        regroup(0)
-        for i in range(GROUPS + 2):
-            run(head_root, i - 1)
-            run(row_stats, i + 2)
-            run(quantise, i)
-            run(project, i)
+        for i in range(-2, GROUPS + 2):
+            run(row_squares, i + 2, range(0, 1))
+            run(square_head_means, i - 1)
             run(normalise, i + 1)
             run(transpose, i + 1)
-            run(finish, i - 1)
-            run(head_stats, i)
+            run(head_mean_squares, i - 1)
+            run(quantise, i)
+            run(project, i)
+            run(head_root, i - 1)
+            run(row_squares, i + 2, range(1, GROUP))
+            run(row_root, i + 2)
+            run(invert_head_rms, i - 1)
+            run(store_v, i - 1)
+            run(store_q, i - 1)
+            run(head_moments, i)
+            run(invert_row_rms, i + 2)
+            run(store_k, i - 1)
             run(regroup, i + 1)
-            run(store_v, i)

@@ -41,6 +41,11 @@ def tile_flashinfer_normqknorm_pa_t_kernel(tc, X, W_q, W_k, W_v, out_0, out_1, o
         psum = ctx.enter_context(tc.psum_pool(name="psum", bufs=2))
         ctx.enter_context(tc.manual_schedule())
 
+        one = const.tile([P, 1], F32)
+        nc.vector.memset(one[:], 1.0)
+        root_of_one = const.tile([P, 1], F32)
+        nc.scalar.activation(out=root_of_one[:], in_=one[:], func=ACT.Sqrt)
+
         ident = const.tile([P, P], F32)
         make_identity(nc, ident[:])
 

@@ -37,7 +37,7 @@ def tile_flashinfer_normqknorm_pa_t_kernel(tc, X, W_q, W_k, W_v, out_0, out_1, o
         xin = ctx.enter_context(tc.tile_pool(name="xin", bufs=GROUPS))
         work = ctx.enter_context(tc.tile_pool(name="work", bufs=2))
         small = ctx.enter_context(tc.tile_pool(name="small", bufs=3))
-        outs = ctx.enter_context(tc.tile_pool(name="outs", bufs=4))
+        outs = ctx.enter_context(tc.tile_pool(name="outs", bufs=GROUPS))
         psum = ctx.enter_context(tc.psum_pool(name="psum", bufs=2))
         ctx.enter_context(tc.manual_schedule())
 
@@ -49,7 +49,7 @@ def tile_flashinfer_normqknorm_pa_t_kernel(tc, X, W_q, W_k, W_v, out_0, out_1, o
         ident = const.tile([P, P], F32)
         make_identity(nc, ident[:])
 
-        x_sb, squares, sum_sq, rms, inv_rms, xn, xt, grouped = {}, {}, {}, {}, {}, {}, {}, {}
+        x_sb, sum_sq, rms, inv_rms, xn, xt, grouped = {}, {}, {}, {}, {}, {}, {}
         x_codes, x_scales, acc, moments, mean_sq, head_ms, head_rms, head_inv = {}, {}, {}, {}, {}, {}, {}, {}
 
         def load(g):
@@ -76,13 +76,12 @@ def tile_flashinfer_normqknorm_pa_t_kernel(tc, X, W_q, W_k, W_v, out_0, out_1, o
                 in_=w_grouped[:, w, :, :].rearrange("p n t -> p (n t)"),
             )
 
-        def row_squares(g, tiles):
-            if g not in sum_sq:
-                squares[g] = work.tile([P, GROUP, FEATURES], BF16, name="squares")
-                sum_sq[g] = small.tile([P, GROUP], F32, name="sum_sq")
-            for j in tiles:
+        def row_squares(g):
+            squares = work.tile([P, GROUP, FEATURES], BF16, name="squares")
+            sum_sq[g] = small.tile([P, GROUP], F32, name="sum_sq")
+            for j in range(GROUP):
                 nc.scalar.activation(
-                    out=squares[g][:, j, :], in_=x_sb[g][:, j, :], func=ACT.Square,
+                    out=squares[:, j, :], in_=x_sb[g][:, j, :], func=ACT.Square,
                     accum_out=sum_sq[g][:, j : j + 1],
                 )
 
@@ -130,8 +129,8 @@ def tile_flashinfer_normqknorm_pa_t_kernel(tc, X, W_q, W_k, W_v, out_0, out_1, o
 
         def project(g):
             acc[g] = []
-            for w, name in enumerate(("acc_q", "acc_k", "acc_v")):
-                bank = psum.tile([P, GROUP, HEADS, HEAD_DIM], F32, name=name)
+            for w, (name, bufs) in enumerate((("acc_q", 2), ("acc_k", 3), ("acc_v", 1))):
+                bank = psum.tile([P, GROUP, HEADS, HEAD_DIM], F32, name=name, bufs=bufs)
                 for j in range(GROUP):
                     nc.tensor.matmul_mx(
                         out=bank[:, j, :, :].rearrange("p h d -> p (h d)"),
@@ -199,25 +198,24 @@ def tile_flashinfer_normqknorm_pa_t_kernel(tc, X, W_q, W_k, W_v, out_0, out_1, o
             nc.vector.tensor_copy(out=v_sb[:].rearrange("p h j d -> p j h d"), in_=acc[g][2][:])
             nc.sync.dma_start(out=v_rows[:, :, g * GROUP : (g + 1) * GROUP, :], in_=v_sb[:])
 
-        def run(stage, g, *args):
+        def run(stage, g):
             if 0 <= g < GROUPS:
-                stage(g, *args)
+                stage(g)
 
         for i in range(-2, GROUPS + 2):
-            run(row_squares, i + 2, range(0, 1))
-            run(square_head_means, i - 1)
+            run(row_squares, i + 2)
+            run(head_moments, i - 1)
             run(normalise, i + 1)
             run(transpose, i + 1)
+            run(square_head_means, i - 1)
+            run(store_v, i - 1)
             run(head_mean_squares, i - 1)
             run(quantise, i)
             run(project, i)
             run(head_root, i - 1)
-            run(row_squares, i + 2, range(1, GROUP))
             run(row_root, i + 2)
             run(invert_head_rms, i - 1)
-            run(store_v, i - 1)
-            run(store_q, i - 1)
-            run(head_moments, i)
             run(invert_row_rms, i + 2)
-            run(store_k, i - 1)
+            run(store_k, i - 2)
+            run(store_q, i - 1)
             run(regroup, i + 1)

from contextlib import ExitStack

import concourse.mybir as mybir
from concourse.masks import make_identity

BF16 = mybir.dt.bfloat16
F32 = mybir.dt.float32
U32 = mybir.dt.uint32
U8 = mybir.dt.uint8
FP8X4 = mybir.dt.float8_e4m3fn_x4
ACT = mybir.ActivationFunctionType
ALU = mybir.AluOpType

P = 128
ROWS = 8192
FEATURES = 512
HEADS = 2
HEAD_DIM = 64
WIDTH = HEADS * HEAD_DIM
TILES = ROWS // P
GROUP = 4
GROUPS = TILES // GROUP
PAIR = 2

FLOPS = 2 * ROWS * FEATURES * 3 * WIDTH


def tile_flashinfer_normqknorm_pa_t_kernel(tc, X, W_q, W_k, W_v, out_0, out_1, out_2):
    nc = tc.nc
    x_rows = X.rearrange("(p t) k -> p t k", t=TILES)
    q_rows = out_0.rearrange("(p t) h d -> p t (h d)", t=TILES)
    k_rows = out_1.rearrange("h (p t) d -> p h t d", t=TILES)
    v_rows = out_2.rearrange("h (p t) d -> p h t d", t=TILES)

    with ExitStack() as ctx:
        const = ctx.enter_context(tc.tile_pool(name="const", bufs=1))
        xin = ctx.enter_context(tc.tile_pool(name="xin", bufs=GROUPS))
        work = ctx.enter_context(tc.tile_pool(name="work", bufs=2))
        small = ctx.enter_context(tc.tile_pool(name="small", bufs=3))
        outs = ctx.enter_context(tc.tile_pool(name="outs", bufs=GROUPS))
        psum = ctx.enter_context(tc.psum_pool(name="psum", bufs=2))
        ctx.enter_context(tc.manual_schedule())

        one = const.tile([P, 1], F32)
        nc.vector.memset(one[:], 1.0)
        root_of_one = const.tile([P, 1], F32)
        nc.scalar.activation(out=root_of_one[:], in_=one[:], func=ACT.Sqrt)

        ident = const.tile([P, P], F32)
        make_identity(nc, ident[:])

        x_sb, sum_sq, rms, inv_rms, xn, xt, grouped = {}, {}, {}, {}, {}, {}, {}
        x_codes, x_scales, acc, moments, mean_sq, head_ms, head_rms, head_inv = {}, {}, {}, {}, {}, {}, {}, {}

        def load(g):
            x_sb[g] = xin.tile([P, GROUP, FEATURES], BF16, name="x_sb")
            nc.sync.dma_start(out=x_sb[g][:], in_=x_rows[:, g * GROUP : (g + 1) * GROUP, :])

        load(0)
        w_raw = const.tile([P, 3, 4, WIDTH], BF16)
        for w, weight in enumerate((W_q, W_k, W_v)):
            nc.sync.dma_start(
                out=w_raw[:, w, :, :].rearrange("p (u e) n -> p u e n", u=2),
                in_=weight.rearrange("(u p e) n -> p u e n", u=2, e=2),
            )
        for g in range(1, GROUPS):
            load(g)
        w_grouped = const.tile([P, 3, WIDTH, 4], BF16, align_bytes=64)
        nc.vector.tensor_copy(out=w_grouped[:], in_=w_raw[:].rearrange("p w t n -> p w n t"))
        w_codes = const.tile([P, 3, WIDTH], U32, align_bytes=64)
        w_scales = const.tile([P, 3, WIDTH], U8, align_bytes=64)
        for w in range(3):
            nc.vector.quantize_mx(
                out=w_codes[:, w, :].bitcast(FP8X4),
                scales=w_scales[:, w, :],
                in_=w_grouped[:, w, :, :].rearrange("p n t -> p (n t)"),
            )

        def row_squares(g):
            squares = work.tile([P, GROUP, FEATURES], BF16, name="squares")
            sum_sq[g] = small.tile([P, GROUP], F32, name="sum_sq")
            for j in range(GROUP):
                nc.scalar.activation(
                    out=squares[:, j, :], in_=x_sb[g][:, j, :], func=ACT.Square,
                    accum_out=sum_sq[g][:, j : j + 1],
                )

        def row_root(g):
            rms[g] = small.tile([P, GROUP], F32, name="rms")
            nc.scalar.activation(out=rms[g][:], in_=sum_sq[g][:], func=ACT.Sqrt, scale=1.0 / FEATURES)

        def invert_row_rms(g):
            inv_rms[g] = small.tile([P, GROUP], F32, name="inv_rms")
            nc.vector.reciprocal(out=inv_rms[g][:], in_=rms[g][:])

        def normalise(g):
            xn[g] = work.tile([P, GROUP, FEATURES], BF16, name="xn")
            for j in range(GROUP):
                nc.vector.tensor_scalar_mul(
                    out=xn[g][:, j, :], in0=x_sb[g][:, j, :], scalar1=inv_rms[g][:, j : j + 1]
                )

        def transpose(g):
            xt[g] = []
            for j0 in range(0, GROUP, PAIR):
                bank = psum.tile([P, PAIR, 2, P], F32, name="xt")
                for jj in range(PAIR):
                    words = xn[g][:, j0 + jj, :].bitcast(F32)
                    for u in range(2):
                        nc.tensor.transpose(bank[:, jj, u, :], words[:, u * P : (u + 1) * P], ident[:])
                xt[g].append(bank)

        def regroup(g):
            grouped[g] = work.tile([P, GROUP, P, 4], BF16, name="grouped", align_bytes=64)
            for b, bank in enumerate(xt[g]):
                nc.scalar.copy(
                    out=grouped[g][:, b * PAIR : (b + 1) * PAIR, :, :].bitcast(F32),
                    in_=bank[:].rearrange("p j u r -> p j r u"),
                )

        def quantise(g):
            x_codes[g] = work.tile([P, GROUP, P], U32, name="x_codes", align_bytes=64)
            x_scales[g] = work.tile([P, GROUP, P], U8, name="x_scales", align_bytes=64)
            nc.vector.quantize_mx(
                out=x_codes[g][:].rearrange("p j r -> p (j r)").bitcast(FP8X4),
                scales=x_scales[g][:].rearrange("p j r -> p (j r)"),
                in_=grouped[g][:].rearrange("p j r t -> p (j r t)"),
            )

        def project(g):
            acc[g] = []
            for w, (name, bufs) in enumerate((("acc_q", 2), ("acc_k", 3), ("acc_v", 1))):
                bank = psum.tile([P, GROUP, HEADS, HEAD_DIM], F32, name=name, bufs=bufs)
                for j in range(GROUP):
                    nc.tensor.matmul_mx(
                        out=bank[:, j, :, :].rearrange("p h d -> p (h d)"),
                        lhsT=x_codes[g][:, j, :].bitcast(FP8X4),
                        lhsT_scale=x_scales[g][:, j, :],
                        rhs=w_codes[:, w, :].bitcast(FP8X4),
                        rhs_scale=w_scales[:, w, :],
                        start=True,
                        stop=True,
                    )
                acc[g].append(bank)

        def head_moments(g):
            moments[g] = small.tile([P, 2, GROUP, HEADS, 3], F32, name="moments")
            for a in range(2):
                for j in range(GROUP):
                    nc.vector.bn_stats(
                        out=moments[g][:, a, j, :, :].rearrange("p h s -> p (h s)"),
                        in_=acc[g][a][:, j, :, :].rearrange("p h d -> p d h"),
                    )

        def square_head_means(g):
            mean = moments[g][:, :, :, :, 1]
            mean_sq[g] = small.tile([P, 2, GROUP, HEADS], F32, name="mean_sq")
            nc.vector.tensor_tensor(out=mean_sq[g][:], in0=mean, in1=mean, op=ALU.mult)

        def head_mean_squares(g):
            head_ms[g] = small.tile([P, 2, GROUP, HEADS], F32, name="head_ms")
            nc.vector.scalar_tensor_tensor(
                out=head_ms[g][:], in0=moments[g][:, :, :, :, 2], scalar=1.0 / HEAD_DIM,
                in1=mean_sq[g][:], op0=ALU.mult, op1=ALU.add,
            )

        def head_root(g):
            head_rms[g] = small.tile([P, 2, GROUP, HEADS], F32, name="head_rms")
            nc.scalar.activation(out=head_rms[g][:], in_=head_ms[g][:], func=ACT.Sqrt)

        def invert_head_rms(g):
            head_inv[g] = small.tile([P, 2, GROUP, HEADS], F32, name="head_inv")
            nc.vector.reciprocal(out=head_inv[g][:], in_=head_rms[g][:])

        def store_q(g):
            q_sb = outs.tile([P, GROUP, HEADS, HEAD_DIM], F32, name="q_sb")
            nc.vector.tensor_tensor(
                out=q_sb[:], in0=acc[g][0][:],
                in1=head_inv[g][:, 0].unsqueeze(3).to_broadcast([P, GROUP, HEADS, HEAD_DIM]),
                op=ALU.mult,
            )
            nc.sync.dma_start(
                out=q_rows[:, g * GROUP : (g + 1) * GROUP, :],
                in_=q_sb[:].rearrange("p j h d -> p j (h d)"),
            )

        def store_k(g):
            k_sb = outs.tile([P, HEADS, GROUP, HEAD_DIM], F32, name="k_sb")
            nc.vector.tensor_tensor(
                out=k_sb[:].rearrange("p h j d -> p j h d"), in0=acc[g][1][:],
                in1=head_inv[g][:, 1].unsqueeze(3).to_broadcast([P, GROUP, HEADS, HEAD_DIM]),
                op=ALU.mult,
            )
            nc.sync.dma_start(out=k_rows[:, :, g * GROUP : (g + 1) * GROUP, :], in_=k_sb[:])

        def store_v(g):
            v_sb = outs.tile([P, HEADS, GROUP, HEAD_DIM], F32, name="v_sb")
            nc.vector.tensor_copy(out=v_sb[:].rearrange("p h j d -> p j h d"), in_=acc[g][2][:])
            nc.sync.dma_start(out=v_rows[:, :, g * GROUP : (g + 1) * GROUP, :], in_=v_sb[:])

        def run(stage, g):
            if 0 <= g < GROUPS:
                stage(g)

        for i in range(-2, GROUPS + 2):
            run(row_squares, i + 2)
            run(head_moments, i - 1)
            run(normalise, i + 1)
            run(transpose, i + 1)
            run(square_head_means, i - 1)
            run(store_v, i - 1)
            run(head_mean_squares, i - 1)
            run(quantise, i)
            run(project, i)
            run(head_root, i - 1)
            run(row_root, i + 2)
            run(invert_head_rms, i - 1)
            run(invert_row_rms, i + 2)
            run(store_k, i - 2)
            run(store_q, i - 1)
            run(regroup, i + 1)
